import numpy as np
import ml_dtypes


def mxq(x, axis, fmt="e4m3"):
    dtype, down = {"e4m3": (ml_dtypes.float8_e4m3fn, 7), "e5m2": (ml_dtypes.float8_e5m2, 14)}[fmt]
    v = np.moveaxis(np.asarray(x, np.float32).astype(ml_dtypes.bfloat16).astype(np.float64), axis, -1)
    blocks = v.reshape(v.shape[:-1] + (-1, 32))
    amax = np.abs(blocks).max(-1, keepdims=True)
    byte = np.maximum(np.where(amax > 0, np.frexp(amax)[1] - 1 + 127, 0) - down, 1)
    scale = np.exp2(byte - 127.0)
    codes = (blocks / scale).astype(np.float32).astype(dtype).astype(np.float64)
    return np.moveaxis((codes * scale).reshape(v.shape), -1, axis)


WIDE = False


def mx_kscale(k):
    if not WIDE:
        return np.ones(k)
    levels = np.array([10, -10, 5, -5, 0])
    a = np.random.permutation(np.resize(levels, k // 512 * 4)).reshape(k // 512, 4)
    idx = np.arange(k)
    return np.exp2(a[idx // 512, idx % 128 // 32])


BF16 = ml_dtypes.bfloat16


def bf(x):
    return np.asarray(x, np.float32).astype(BF16)


def f64(x):
    return np.asarray(x).astype(np.float64)


B, S, D, DI = 4, 2048, 512, 512
EPS = 1e-12
KV_RMS = np.sqrt(S * (S / D + 1.0) / DI)


def l2norm(v):
    n = np.sqrt(np.sum(v * v, axis=-1, keepdims=True))
    return v / np.maximum(n, EPS)


def setup_inputs():
    t = mx_kscale(DI)
    return {"x": bf(np.random.standard_normal((B, S, D))),
            "wq": bf(np.random.standard_normal((D, DI)) / np.sqrt(D)),
            "kv": bf(np.random.standard_normal((B, 1, DI)) * KV_RMS * t),
            "wo": bf(np.random.standard_normal((DI, D)) / KV_RMS / t[:, None])}


def reference(x, wq, kv, wo):
    xf = f64(x)
    q = l2norm(mxq(xf, 2, "e4m3") @ mxq(f64(wq), 0, "e4m3"))
    g = q * f64(kv)
    return (mxq(g, 2, "e4m3") @ mxq(f64(wo), 0, "e4m3")) + xf

@@ -1,0 +1,209 @@
+from contextlib import ExitStack
+
+import concourse.mybir as mybir
+from concourse.masks import make_identity
+
+F32 = mybir.dt.float32
+BF16 = mybir.dt.bfloat16
+U32 = mybir.dt.uint32
+U8 = mybir.dt.uint8
+FP8X4 = mybir.dt.float8_e4m3fn_x4
+ACT = mybir.ActivationFunctionType
+ALU = mybir.AluOpType
+
+B, S, D, DI = 4, 2048, 512, 512
+EPS = 1e-12
+FLOPS = 2 * B * S * D * DI + 2 * B * S * DI * D
+
+P = 128
+PACK = 4
+HALVES = 2
+TILES_PER_BATCH = S // P
+UNIT_TILES = 2
+UNIT_TOKENS = UNIT_TILES * P
+UNITS = B * S // UNIT_TOKENS
+
+ROOT_FLOOR = 2.0 ** -112
+
+
+def tile_hydraencoderlayer_pb_t_kernel(tc, x, wq, kv, wo, out):
+    nc = tc.nc
+    x_rows = x.flatten_outer_dims()
+    out_rows = out.flatten_outer_dims()
+
+    def unit_rows(rows, u):
+        b, first_tile = divmod(u * UNIT_TILES, TILES_PER_BATCH)
+        batch = rows[b * S : (b + 1) * S, :].rearrange("(p t) d -> p t d", t=TILES_PER_BATCH)
+        return batch[:, first_tile : first_tile + UNIT_TILES, :]
+
+    with ExitStack() as stack:
+        stack.enter_context(tc.manual_schedule())
+        keep = stack.enter_context(tc.tile_pool(name="keep", bufs=1))
+        stream = stack.enter_context(tc.tile_pool(name="stream", bufs=3))
+        results = stack.enter_context(tc.tile_pool(name="results", bufs=4))
+        words_psum = stack.enter_context(tc.psum_pool(name="words_psum", bufs=2))
+        a_psum = stack.enter_context(tc.psum_pool(name="a_psum", bufs=2 * UNIT_TILES))
+        o_psum = stack.enter_context(tc.psum_pool(name="o_psum", bufs=UNIT_TILES))
+
+        def load_weight(w, name):
+            raw = keep.tile([P, PACK, w.shape[1]], BF16, name=name)
+            nc.sync.dma_start(
+                out=raw[:].rearrange("p (h e) n -> p h (e n)", h=HALVES),
+                in_=w.rearrange("(h p e) n -> p h (e n)", h=HALVES, p=P),
+            )
+            return raw
+
+        kv_all = keep.tile([P, B * DI], BF16, name="kv_all")
+        nc.scalar.dma_start(
+            out=kv_all[:], in_=kv.rearrange("b o e -> (b o e)").partition_broadcast(P)
+        )
+        x_sb = {}
+
+        def load_x(u):
+            x_unit = keep.tile([P, UNIT_TILES, D], BF16, name="x%d" % u)
+            nc.sync.dma_start(out=x_unit[:], in_=unit_rows(x_rows, u))
+            x_sb[u] = x_unit
+
+        wq_raw = load_weight(wq, "wq_raw")
+        load_x(0)
+        load_x(1)
+        wo_raw = load_weight(wo, "wo_raw")
+        for u in range(2, UNITS):
+            load_x(u)
+
+        identity = keep.tile([P, P], F32, name="identity")
+        make_identity(nc, identity[:])
+        one = keep.tile([P, 1], F32, name="one")
+        nc.vector.memset(one[:], 1.0)
+        nc.scalar.activation(out=one[:], in_=one[:], func=ACT.Sqrt)
+
+        def quantise_weight(raw, name):
+            n = raw.shape[2]
+            grouped = keep.tile([P, n, PACK], BF16, name=name + "_grouped", align_bytes=64)
+            nc.vector.tensor_copy(out=grouped[:], in_=raw[:].rearrange("p t n -> p n t"))
+            codes = keep.tile([P, n], U32, name=name + "_codes", align_bytes=64)
+            scales = keep.tile([P, n], U8, name=name + "_scales", align_bytes=64)
+            nc.vector.quantize_mx(
+                out=codes[:].bitcast(FP8X4),
+                scales=scales[:],
+                in_=grouped[:].rearrange("p n t -> p (n t)"),
+            )
+            return codes, scales
+
+        grouped_of = {}
+        mx_of = {}
+        a_of, root_of, inv_norm_of, g_of, o_of = {}, {}, {}, {}, {}
+
+        def transpose_unit(kind, u, rows_sb):
+            words = rows_sb[:].bitcast(F32)
+            bank = words_psum.tile([P, HALVES, UNIT_TOKENS], F32, tag="words")
+            for i in range(UNIT_TILES):
+                for h in range(HALVES):
+                    nc.tensor.transpose(
+                        bank[:, h, i * P : (i + 1) * P], words[:, i, h * P : (h + 1) * P], identity[:]
+                    )
+            grouped = stream.tile([P, UNIT_TOKENS * PACK], BF16, tag=kind + "_grouped", align_bytes=64)
+            nc.scalar.copy(
+                out=grouped[:].bitcast(F32).rearrange("p (c h) -> p c h", h=HALVES),
+                in_=bank[:].rearrange("p h c -> p c h"),
+            )
+            grouped_of[kind, u] = grouped
+
+        def quantise_unit(kind, u):
+            codes = stream.tile([P, UNIT_TOKENS], U32, tag=kind + "_codes", align_bytes=64)
+            scales = stream.tile([P, UNIT_TOKENS], U8, tag=kind + "_scales", align_bytes=64)
+            nc.vector.quantize_mx(
+                out=codes[:].bitcast(FP8X4), scales=scales[:], in_=grouped_of[kind, u][:]
+            )
+            mx_of[kind, u] = (codes, scales)
+
+        def multiply_unit(kind, u, weight, psum_pool, tag):
+            codes, scales = mx_of[kind, u]
+            w_codes, w_scales = weight
+            banks = []
+            for i in range(UNIT_TILES):
+                tokens = slice(i * P, (i + 1) * P)
+                acc = psum_pool.tile([P, w_codes.shape[1]], F32, tag=tag)
+                nc.tensor.matmul_mx(
+                    out=acc[:],
+                    lhsT=codes[:, tokens].bitcast(FP8X4),
+                    lhsT_scale=scales[:, tokens],
+                    rhs=w_codes[:].bitcast(FP8X4),
+                    rhs_scale=w_scales[:],
+                    start=True,
+                    stop=True,
+                )
+                banks.append(acc)
+            return banks
+
+        def norms(u):
+            sums = stream.tile([P, UNIT_TILES], F32, tag="sums")
+            for i in range(UNIT_TILES):
+                squares = stream.tile([P, DI], BF16, tag="squares")
+                nc.scalar.activation(
+                    out=squares[:], in_=a_of[u][i][:], func=ACT.Square, accum_out=sums[:, i : i + 1]
+                )
+            root = stream.tile([P, UNIT_TILES], F32, tag="root")
+            nc.scalar.activation(out=root[:], in_=sums[:], func=ACT.Sqrt, bias=ROOT_FLOOR)
+            root_of[u] = root
+
+        def clamp_norms(u):
+            nc.vector.tensor_scalar_max(out=root_of[u][:], in0=root_of[u][:], scalar1=EPS)
+
+        def invert_norms(u):
+            inv_norm = stream.tile([P, UNIT_TILES], F32, tag="inv_norm")
+            nc.vector.reciprocal(out=inv_norm[:], in_=root_of[u][:])
+            inv_norm_of[u] = inv_norm
+
+        def gate(u):
+            b = u * UNIT_TOKENS // S
+            g = stream.tile([P, UNIT_TILES, DI], BF16, tag="g")
+            for i in range(UNIT_TILES):
+                nc.vector.scalar_tensor_tensor(
+                    out=g[:, i, :],
+                    in0=a_of[u][i][:],
+                    scalar=inv_norm_of[u][:, i : i + 1],
+                    in1=kv_all[:, b * DI : (b + 1) * DI],
+                    op0=ALU.mult,
+                    op1=ALU.mult,
+                )
+            g_of[u] = g
+
+        def finish(u):
+            result = results.tile([P, UNIT_TILES, D], F32, tag="result")
+            for i in range(UNIT_TILES):
+                nc.vector.tensor_tensor(
+                    out=result[:, i, :], in0=o_of[u][i][:], in1=x_sb[u][:, i, :], op=ALU.add
+                )
+            nc.sync.dma_start(out=unit_rows(out_rows, u), in_=result[:])
+
+        def live(u):
+            return 0 <= u < UNITS
+
+        def step(n):
+            if live(n - 2):
+                quantise_unit("g", n - 2)
+                o_of[n - 2] = multiply_unit("g", n - 2, wo_mx, o_psum, "o")
+            if live(n):
+                clamp_norms(n)
+            if live(n + 1):
+                quantise_unit("x", n + 1)
+                a_of[n + 1] = multiply_unit("x", n + 1, wq_mx, a_psum, "a")
+            if live(n):
+                invert_norms(n)
+            if live(n + 1):
+                norms(n + 1)
+            if live(n + 3):
+                transpose_unit("x", n + 3, x_sb[n + 3])
+            if live(n):
+                gate(n)
+                transpose_unit("g", n, g_of[n])
+            if live(n - 2):
+                finish(n - 2)
+
+        wq_mx = quantise_weight(wq_raw, "wq")
+        for n in range(-3, 0):
+            step(n)
+        wo_mx = quantise_weight(wo_raw, "wo")
+        for n in range(0, UNITS + 2):
+            step(n)

@@ -22,6 +22,9 @@ TILES_PER_BATCH = S // P
 UNIT_TILES = 2
 UNIT_TOKENS = UNIT_TILES * P
 UNITS = B * S // UNIT_TOKENS
+AHEAD = 3
+X_HALF = 0
+G_HALF = 1
 
 ROOT_FLOOR = 2.0 ** -112
 
@@ -90,11 +93,13 @@ def tile_hydraencoderlayer_pb_t_kernel(tc, x, wq, kv, wo, out):
             )
             return codes, scales
 
-        grouped_of = {}
-        mx_of = {}
-        a_of, root_of, inv_norm_of, g_of, o_of = {}, {}, {}, {}, {}
+        grouped_of, mx_of = {}, {}
+        a_of, root_of, inv_norm_of, g_of, o_of, result_of = {}, {}, {}, {}, {}, {}
 
-        def transpose_unit(kind, u, rows_sb):
+        def live(u):
+            return 0 <= u < UNITS
+
+        def transpose_unit(rows_sb, grouped_half):
             words = rows_sb[:].bitcast(F32)
             bank = words_psum.tile([P, HALVES, UNIT_TOKENS], F32, tag="words")
             for i in range(UNIT_TILES):
@@ -102,23 +107,32 @@ def tile_hydraencoderlayer_pb_t_kernel(tc, x, wq, kv, wo, out):
                     nc.tensor.transpose(
                         bank[:, h, i * P : (i + 1) * P], words[:, i, h * P : (h + 1) * P], identity[:]
                     )
-            grouped = stream.tile([P, UNIT_TOKENS * PACK], BF16, tag=kind + "_grouped", align_bytes=64)
             nc.scalar.copy(
-                out=grouped[:].bitcast(F32).rearrange("p (c h) -> p c h", h=HALVES),
+                out=grouped_half.bitcast(F32).rearrange("p (c h) -> p c h", h=HALVES),
                 in_=bank[:].rearrange("p h c -> p c h"),
             )
-            grouped_of[kind, u] = grouped
 
-        def quantise_unit(kind, u):
-            codes = stream.tile([P, UNIT_TOKENS], U32, tag=kind + "_codes", align_bytes=64)
-            scales = stream.tile([P, UNIT_TOKENS], U8, tag=kind + "_scales", align_bytes=64)
+        def transpose_pair(n):
+            grouped = stream.tile([P, 2, UNIT_TOKENS * PACK], BF16, tag="grouped", align_bytes=64)
+            if live(n + AHEAD):
+                transpose_unit(x_sb[n + AHEAD], grouped[:, X_HALF, :])
+            if live(n):
+                transpose_unit(g_of[n], grouped[:, G_HALF, :])
+            grouped_of[n] = grouped
+
+        def quantise_pair(n):
+            codes = stream.tile([P, 2, UNIT_TOKENS], U32, tag="codes", align_bytes=64)
+            scales = stream.tile([P, 2, UNIT_TOKENS], U8, tag="scales", align_bytes=64)
+            filled = slice(X_HALF if live(n + AHEAD) else G_HALF, G_HALF + 1 if live(n) else G_HALF)
             nc.vector.quantize_mx(
-                out=codes[:].bitcast(FP8X4), scales=scales[:], in_=grouped_of[kind, u][:]
+                out=codes[:, filled, :].rearrange("p s c -> p (s c)").bitcast(FP8X4),
+                scales=scales[:, filled, :].rearrange("p s c -> p (s c)"),
+                in_=grouped_of[n][:, filled, :].rearrange("p s c -> p (s c)"),
             )
-            mx_of[kind, u] = (codes, scales)
+            mx_of[n] = (codes, scales)
 
-        def multiply_unit(kind, u, weight, psum_pool, tag):
-            codes, scales = mx_of[kind, u]
+        def multiply_unit(operand, half, weight, psum_pool, tag):
+            codes, scales = operand
             w_codes, w_scales = weight
             banks = []
             for i in range(UNIT_TILES):
@@ -126,8 +140,8 @@ def tile_hydraencoderlayer_pb_t_kernel(tc, x, wq, kv, wo, out):
                 acc = psum_pool.tile([P, w_codes.shape[1]], F32, tag=tag)
                 nc.tensor.matmul_mx(
                     out=acc[:],
-                    lhsT=codes[:, tokens].bitcast(FP8X4),
-                    lhsT_scale=scales[:, tokens],
+                    lhsT=codes[:, half, tokens].bitcast(FP8X4),
+                    lhsT_scale=scales[:, half, tokens],
                     rhs=w_codes[:].bitcast(FP8X4),
                     rhs_scale=w_scales[:],
                     start=True,
@@ -169,40 +183,44 @@ def tile_hydraencoderlayer_pb_t_kernel(tc, x, wq, kv, wo, out):
                 )
             g_of[u] = g
 
-        def finish(u):
+        def add_x_beside_vector(u, i):
             result = results.tile([P, UNIT_TILES, D], F32, tag="result")
-            for i in range(UNIT_TILES):
-                nc.vector.tensor_tensor(
-                    out=result[:, i, :], in0=o_of[u][i][:], in1=x_sb[u][:, i, :], op=ALU.add
-                )
-            nc.sync.dma_start(out=unit_rows(out_rows, u), in_=result[:])
+            nc.scalar.copy(out=result[:, i, :], in_=o_of[u][i][:])
+            nc.gpsimd.tensor_tensor(
+                out=result[:, i, :], in0=result[:, i, :], in1=x_sb[u][:, i, :], op=ALU.add
+            )
+            result_of[u] = result
 
-        def live(u):
-            return 0 <= u < UNITS
+        def add_x_on_vector(u, i):
+            nc.vector.tensor_tensor(
+                out=result_of[u][:, i, :], in0=o_of[u][i][:], in1=x_sb[u][:, i, :], op=ALU.add
+            )
 
         def step(n):
-            if live(n - 2):
-                quantise_unit("g", n - 2)
-                o_of[n - 2] = multiply_unit("g", n - 2, wo_mx, o_psum, "o")
             if live(n):
                 clamp_norms(n)
+            if live(n - 2) or live(n + 1):
+                quantise_pair(n - 2)
+            if live(n - 2):
+                o_of[n - 2] = multiply_unit(mx_of[n - 2], G_HALF, wo_mx, o_psum, "o")
             if live(n + 1):
-                quantise_unit("x", n + 1)
-                a_of[n + 1] = multiply_unit("x", n + 1, wq_mx, a_psum, "a")
+                a_of[n + 1] = multiply_unit(mx_of[n - 2], X_HALF, wq_mx, a_psum, "a")
+            if live(n - 2):
+                add_x_beside_vector(n - 2, 0)
             if live(n):
                 invert_norms(n)
             if live(n + 1):
                 norms(n + 1)
-            if live(n + 3):
-                transpose_unit("x", n + 3, x_sb[n + 3])
             if live(n):
                 gate(n)
-                transpose_unit("g", n, g_of[n])
+            if live(n) or live(n + AHEAD):
+                transpose_pair(n)
             if live(n - 2):
-                finish(n - 2)
+                add_x_on_vector(n - 2, 1)
+                nc.sync.dma_start(out=unit_rows(out_rows, n - 2), in_=result_of[n - 2][:])
 
         wq_mx = quantise_weight(wq_raw, "wq")
-        for n in range(-3, 0):
+        for n in range(-AHEAD, 0):
             step(n)
         wo_mx = quantise_weight(wo_raw, "wo")
         for n in range(0, UNITS + 2):

@@ -22,7 +22,8 @@ TILES_PER_BATCH = S // P
 UNIT_TILES = 2
 UNIT_TOKENS = UNIT_TILES * P
 UNITS = B * S // UNIT_TOKENS
-AHEAD = 3
+X_AHEAD = 3
+G_BEHIND = 1
 X_HALF = 0
 G_HALF = 1
 
@@ -94,7 +95,7 @@ def tile_hydraencoderlayer_pb_t_kernel(tc, x, wq, kv, wo, out):
             return codes, scales
 
         grouped_of, mx_of = {}, {}
-        a_of, root_of, inv_norm_of, g_of, o_of, result_of = {}, {}, {}, {}, {}, {}
+        a_of, root_of, inv_norm_of, g_of, o_of = {}, {}, {}, {}, {}
 
         def live(u):
             return 0 <= u < UNITS
@@ -114,16 +115,18 @@ def tile_hydraencoderlayer_pb_t_kernel(tc, x, wq, kv, wo, out):
 
         def transpose_pair(n):
             grouped = stream.tile([P, 2, UNIT_TOKENS * PACK], BF16, tag="grouped", align_bytes=64)
-            if live(n + AHEAD):
-                transpose_unit(x_sb[n + AHEAD], grouped[:, X_HALF, :])
-            if live(n):
-                transpose_unit(g_of[n], grouped[:, G_HALF, :])
+            if live(n - G_BEHIND):
+                transpose_unit(g_of[n - G_BEHIND], grouped[:, G_HALF, :])
+            if live(n + X_AHEAD):
+                transpose_unit(x_sb[n + X_AHEAD], grouped[:, X_HALF, :])
             grouped_of[n] = grouped
 
         def quantise_pair(n):
             codes = stream.tile([P, 2, UNIT_TOKENS], U32, tag="codes", align_bytes=64)
             scales = stream.tile([P, 2, UNIT_TOKENS], U8, tag="scales", align_bytes=64)
-            filled = slice(X_HALF if live(n + AHEAD) else G_HALF, G_HALF + 1 if live(n) else G_HALF)
+            first = X_HALF if live(n + X_AHEAD) else G_HALF
+            last = G_HALF if live(n - G_BEHIND) else X_HALF
+            filled = slice(first, last + 1)
             nc.vector.quantize_mx(
                 out=codes[:, filled, :].rearrange("p s c -> p (s c)").bitcast(FP8X4),
                 scales=scales[:, filled, :].rearrange("p s c -> p (s c)"),
@@ -183,45 +186,39 @@ def tile_hydraencoderlayer_pb_t_kernel(tc, x, wq, kv, wo, out):
                 )
             g_of[u] = g
 
-        def add_x_beside_vector(u, i):
+        def finish(u):
             result = results.tile([P, UNIT_TILES, D], F32, tag="result")
-            nc.scalar.copy(out=result[:, i, :], in_=o_of[u][i][:])
-            nc.gpsimd.tensor_tensor(
-                out=result[:, i, :], in0=result[:, i, :], in1=x_sb[u][:, i, :], op=ALU.add
-            )
-            result_of[u] = result
+            for i in range(UNIT_TILES):
+                nc.vector.tensor_tensor(
+                    out=result[:, i, :], in0=o_of[u][i][:], in1=x_sb[u][:, i, :], op=ALU.add
+                )
+            nc.sync.dma_start(out=unit_rows(out_rows, u), in_=result[:])
 
-        def add_x_on_vector(u, i):
-            nc.vector.tensor_tensor(
-                out=result_of[u][:, i, :], in0=o_of[u][i][:], in1=x_sb[u][:, i, :], op=ALU.add
-            )
+        def has_pair(n):
+            return live(n + X_AHEAD) or live(n - G_BEHIND)
 
         def step(n):
-            if live(n):
-                clamp_norms(n)
-            if live(n - 2) or live(n + 1):
-                quantise_pair(n - 2)
-            if live(n - 2):
-                o_of[n - 2] = multiply_unit(mx_of[n - 2], G_HALF, wo_mx, o_psum, "o")
             if live(n + 1):
                 a_of[n + 1] = multiply_unit(mx_of[n - 2], X_HALF, wq_mx, a_psum, "a")
-            if live(n - 2):
-                add_x_beside_vector(n - 2, 0)
-            if live(n):
-                invert_norms(n)
-            if live(n + 1):
                 norms(n + 1)
+            if has_pair(n):
+                transpose_pair(n)
+            if live(n - 4):
+                finish(n - 4)
             if live(n):
                 gate(n)
-            if live(n) or live(n + AHEAD):
-                transpose_pair(n)
-            if live(n - 2):
-                add_x_on_vector(n - 2, 1)
-                nc.sync.dma_start(out=unit_rows(out_rows, n - 2), in_=result_of[n - 2][:])
+            if live(n - 3):
+                o_of[n - 3] = multiply_unit(mx_of[n - 2], G_HALF, wo_mx, o_psum, "o")
+            if live(n + 1):
+                clamp_norms(n + 1)
+            if has_pair(n - 1):
+                quantise_pair(n - 1)
+            if live(n + 1):
+                invert_norms(n + 1)
 
         wq_mx = quantise_weight(wq_raw, "wq")
-        for n in range(-AHEAD, 0):
+        for n in range(-X_AHEAD, -1):
             step(n)
         wo_mx = quantise_weight(wo_raw, "wo")
-        for n in range(0, UNITS + 2):
+        for n in range(-1, UNITS + 4):
             step(n)

@@ -27,8 +27,6 @@ G_BEHIND = 1
 X_HALF = 0
 G_HALF = 1
 
-ROOT_FLOOR = 2.0 ** -112
-
 
 def tile_hydraencoderlayer_pb_t_kernel(tc, x, wq, kv, wo, out):
     nc = tc.nc
@@ -77,9 +75,8 @@ def tile_hydraencoderlayer_pb_t_kernel(tc, x, wq, kv, wo, out):
 
         identity = keep.tile([P, P], F32, name="identity")
         make_identity(nc, identity[:])
-        one = keep.tile([P, 1], F32, name="one")
-        nc.vector.memset(one[:], 1.0)
-        nc.scalar.activation(out=one[:], in_=one[:], func=ACT.Sqrt)
+        minus_half = keep.tile([P, UNIT_TILES], F32, name="minus_half")
+        nc.gpsimd.memset(minus_half[:], -0.5)
 
         def quantise_weight(raw, name):
             n = raw.shape[2]
@@ -95,7 +92,7 @@ def tile_hydraencoderlayer_pb_t_kernel(tc, x, wq, kv, wo, out):
             return codes, scales
 
         grouped_of, mx_of = {}, {}
-        a_of, root_of, inv_norm_of, g_of, o_of = {}, {}, {}, {}, {}
+        a_of, inv_norm_of, g_of, o_of = {}, {}, {}, {}
 
         def live(u):
             return 0 <= u < UNITS
@@ -153,23 +150,17 @@ def tile_hydraencoderlayer_pb_t_kernel(tc, x, wq, kv, wo, out):
                 banks.append(acc)
             return banks
 
-        def norms(u):
+        def inverse_norms(u):
             sums = stream.tile([P, UNIT_TILES], F32, tag="sums")
             for i in range(UNIT_TILES):
                 squares = stream.tile([P, DI], BF16, tag="squares")
                 nc.scalar.activation(
                     out=squares[:], in_=a_of[u][i][:], func=ACT.Square, accum_out=sums[:, i : i + 1]
                 )
-            root = stream.tile([P, UNIT_TILES], F32, tag="root")
-            nc.scalar.activation(out=root[:], in_=sums[:], func=ACT.Sqrt, bias=ROOT_FLOOR)
-            root_of[u] = root
-
-        def clamp_norms(u):
-            nc.vector.tensor_scalar_max(out=root_of[u][:], in0=root_of[u][:], scalar1=EPS)
-
-        def invert_norms(u):
+            clamped = stream.tile([P, UNIT_TILES], F32, tag="clamped")
+            nc.gpsimd.tensor_scalar_max(out=clamped[:], in0=sums[:], scalar1=EPS * EPS)
             inv_norm = stream.tile([P, UNIT_TILES], F32, tag="inv_norm")
-            nc.vector.reciprocal(out=inv_norm[:], in_=root_of[u][:])
+            nc.gpsimd.tensor_tensor(out=inv_norm[:], in0=clamped[:], in1=minus_half[:], op=ALU.pow)
             inv_norm_of[u] = inv_norm
 
         def gate(u):
@@ -200,7 +191,7 @@ def tile_hydraencoderlayer_pb_t_kernel(tc, x, wq, kv, wo, out):
         def step(n):
             if live(n + 1):
                 a_of[n + 1] = multiply_unit(mx_of[n - 2], X_HALF, wq_mx, a_psum, "a")
-                norms(n + 1)
+                inverse_norms(n + 1)
             if has_pair(n):
                 transpose_pair(n)
             if live(n - 4):
@@ -209,12 +200,8 @@ def tile_hydraencoderlayer_pb_t_kernel(tc, x, wq, kv, wo, out):
                 gate(n)
             if live(n - 3):
                 o_of[n - 3] = multiply_unit(mx_of[n - 2], G_HALF, wo_mx, o_psum, "o")
-            if live(n + 1):
-                clamp_norms(n + 1)
             if has_pair(n - 1):
                 quantise_pair(n - 1)
-            if live(n + 1):
-                invert_norms(n + 1)
 
         wq_mx = quantise_weight(wq_raw, "wq")
         for n in range(-X_AHEAD, -1):

@@ -196,12 +196,12 @@ def tile_hydraencoderlayer_pb_t_kernel(tc, x, wq, kv, wo, out):
                 transpose_pair(n)
             if live(n - 4):
                 finish(n - 4)
+            if has_pair(n - 1):
+                quantise_pair(n - 1)
             if live(n):
                 gate(n)
             if live(n - 3):
                 o_of[n - 3] = multiply_unit(mx_of[n - 2], G_HALF, wo_mx, o_psum, "o")
-            if has_pair(n - 1):
-                quantise_pair(n - 1)
 
         wq_mx = quantise_weight(wq_raw, "wq")
         for n in range(-X_AHEAD, -1):

@@ -55,10 +55,13 @@ def tile_hydraencoderlayer_pb_t_kernel(tc, x, wq, kv, wo, out):
             )
             return raw
 
-        kv_all = keep.tile([P, B * DI], BF16, name="kv_all")
-        nc.scalar.dma_start(
-            out=kv_all[:], in_=kv.rearrange("b o e -> (b o e)").partition_broadcast(P)
-        )
+        kv_sb = {}
+
+        def load_kv(b):
+            kv_row = keep.tile([P, DI], BF16, name="kv%d" % b)
+            nc.sync.dma_start(out=kv_row[:], in_=kv[b, 0, :].partition_broadcast(P))
+            kv_sb[b] = kv_row
+
         x_sb = {}
 
         def load_x(u):
@@ -66,11 +69,14 @@ def tile_hydraencoderlayer_pb_t_kernel(tc, x, wq, kv, wo, out):
             nc.sync.dma_start(out=x_unit[:], in_=unit_rows(x_rows, u))
             x_sb[u] = x_unit
 
-        wq_raw = load_weight(wq, "wq_raw")
         load_x(0)
+        wq_raw = load_weight(wq, "wq_raw")
         load_x(1)
+        load_kv(0)
         wo_raw = load_weight(wo, "wo_raw")
         for u in range(2, UNITS):
+            if u * UNIT_TOKENS % S == 0:
+                load_kv(u * UNIT_TOKENS // S)
             load_x(u)
 
         identity = keep.tile([P, P], F32, name="identity")
@@ -171,7 +177,7 @@ def tile_hydraencoderlayer_pb_t_kernel(tc, x, wq, kv, wo, out):
                     out=g[:, i, :],
                     in0=a_of[u][i][:],
                     scalar=inv_norm_of[u][:, i : i + 1],
-                    in1=kv_all[:, b * DI : (b + 1) * DI],
+                    in1=kv_sb[b][:],
                     op0=ALU.mult,
                     op1=ALU.mult,
                 )

@@ -24,6 +24,8 @@ UNIT_TOKENS = UNIT_TILES * P
 UNITS = B * S // UNIT_TOKENS
 X_AHEAD = 3
 G_BEHIND = 1
+LOAD_UNITS = 4
+RESULT_BUFS = 24
 X_HALF = 0
 G_HALF = 1
 
@@ -33,16 +35,16 @@ def tile_hydraencoderlayer_pb_t_kernel(tc, x, wq, kv, wo, out):
     x_rows = x.flatten_outer_dims()
     out_rows = out.flatten_outer_dims()
 
-    def unit_rows(rows, u):
+    def unit_rows(rows, u, units=1):
         b, first_tile = divmod(u * UNIT_TILES, TILES_PER_BATCH)
         batch = rows[b * S : (b + 1) * S, :].rearrange("(p t) d -> p t d", t=TILES_PER_BATCH)
-        return batch[:, first_tile : first_tile + UNIT_TILES, :]
+        return batch[:, first_tile : first_tile + units * UNIT_TILES, :]
 
     with ExitStack() as stack:
         stack.enter_context(tc.manual_schedule())
         keep = stack.enter_context(tc.tile_pool(name="keep", bufs=1))
         stream = stack.enter_context(tc.tile_pool(name="stream", bufs=3))
-        results = stack.enter_context(tc.tile_pool(name="results", bufs=4))
+        results = stack.enter_context(tc.tile_pool(name="results", bufs=RESULT_BUFS))
         words_psum = stack.enter_context(tc.psum_pool(name="words_psum", bufs=2))
         a_psum = stack.enter_context(tc.psum_pool(name="a_psum", bufs=2 * UNIT_TILES))
         o_psum = stack.enter_context(tc.psum_pool(name="o_psum", bufs=UNIT_TILES))
@@ -64,20 +66,22 @@ def tile_hydraencoderlayer_pb_t_kernel(tc, x, wq, kv, wo, out):
 
         x_sb = {}
 
-        def load_x(u):
-            x_unit = keep.tile([P, UNIT_TILES, D], BF16, name="x%d" % u)
-            nc.sync.dma_start(out=x_unit[:], in_=unit_rows(x_rows, u))
-            x_sb[u] = x_unit
+        def load_x(u, units=1):
+            x_units = keep.tile([P, units * UNIT_TILES, D], BF16, name="x%d" % u)
+            nc.sync.dma_start(out=x_units[:], in_=unit_rows(x_rows, u, units))
+            for i in range(units):
+                x_sb[u + i] = x_units[:, i * UNIT_TILES : (i + 1) * UNIT_TILES, :]
 
         load_x(0)
         wq_raw = load_weight(wq, "wq_raw")
         load_x(1)
         load_kv(0)
         wo_raw = load_weight(wo, "wo_raw")
-        for u in range(2, UNITS):
+        load_x(2, units=2)
+        for u in range(LOAD_UNITS, UNITS, LOAD_UNITS):
             if u * UNIT_TOKENS % S == 0:
                 load_kv(u * UNIT_TOKENS // S)
-            load_x(u)
+            load_x(u, units=LOAD_UNITS)
 
         identity = keep.tile([P, P], F32, name="identity")
         make_identity(nc, identity[:])
@@ -104,7 +108,7 @@ def tile_hydraencoderlayer_pb_t_kernel(tc, x, wq, kv, wo, out):
             return 0 <= u < UNITS
 
         def transpose_unit(rows_sb, grouped_half):
-            words = rows_sb[:].bitcast(F32)
+            words = rows_sb.bitcast(F32)
             bank = words_psum.tile([P, HALVES, UNIT_TOKENS], F32, tag="words")
             for i in range(UNIT_TILES):
                 for h in range(HALVES):
@@ -119,7 +123,7 @@ def tile_hydraencoderlayer_pb_t_kernel(tc, x, wq, kv, wo, out):
         def transpose_pair(n):
             grouped = stream.tile([P, 2, UNIT_TOKENS * PACK], BF16, tag="grouped", align_bytes=64)
             if live(n - G_BEHIND):
-                transpose_unit(g_of[n - G_BEHIND], grouped[:, G_HALF, :])
+                transpose_unit(g_of[n - G_BEHIND][:], grouped[:, G_HALF, :])
             if live(n + X_AHEAD):
                 transpose_unit(x_sb[n + X_AHEAD], grouped[:, X_HALF, :])
             grouped_of[n] = grouped

@@ -25,7 +25,7 @@ UNITS = B * S // UNIT_TOKENS
 X_AHEAD = 3
 G_BEHIND = 1
 LOAD_UNITS = 4
-RESULT_BUFS = 24
+WARM_UP = 4
 X_HALF = 0
 G_HALF = 1
 
@@ -44,7 +44,7 @@ def tile_hydraencoderlayer_pb_t_kernel(tc, x, wq, kv, wo, out):
         stack.enter_context(tc.manual_schedule())
         keep = stack.enter_context(tc.tile_pool(name="keep", bufs=1))
         stream = stack.enter_context(tc.tile_pool(name="stream", bufs=3))
-        results = stack.enter_context(tc.tile_pool(name="results", bufs=RESULT_BUFS))
+        results = stack.enter_context(tc.tile_pool(name="results", bufs=4))
         words_psum = stack.enter_context(tc.psum_pool(name="words_psum", bufs=2))
         a_psum = stack.enter_context(tc.psum_pool(name="a_psum", bufs=2 * UNIT_TILES))
         o_psum = stack.enter_context(tc.psum_pool(name="o_psum", bufs=UNIT_TILES))
@@ -72,8 +72,8 @@ def tile_hydraencoderlayer_pb_t_kernel(tc, x, wq, kv, wo, out):
             for i in range(units):
                 x_sb[u + i] = x_units[:, i * UNIT_TILES : (i + 1) * UNIT_TILES, :]
 
-        load_x(0)
         wq_raw = load_weight(wq, "wq_raw")
+        load_x(0)
         load_x(1)
         load_kv(0)
         wo_raw = load_weight(wo, "wo_raw")
@@ -87,6 +87,12 @@ def tile_hydraencoderlayer_pb_t_kernel(tc, x, wq, kv, wo, out):
         make_identity(nc, identity[:])
         minus_half = keep.tile([P, UNIT_TILES], F32, name="minus_half")
         nc.gpsimd.memset(minus_half[:], -0.5)
+
+        zeros = keep.tile([P, DI], BF16, name="zeros")
+        nc.vector.memset(zeros[:], 0.0)
+        for i in range(WARM_UP):
+            warm = o_psum.tile([P, DI], F32, name="warm", tag="o")
+            nc.tensor.matmul(warm[:], lhsT=zeros[:, :P], rhs=zeros[:], start=True, stop=True)
 
         def quantise_weight(raw, name):
             n = raw.shape[2]
@@ -193,7 +199,12 @@ def tile_hydraencoderlayer_pb_t_kernel(tc, x, wq, kv, wo, out):
                 nc.vector.tensor_tensor(
                     out=result[:, i, :], in0=o_of[u][i][:], in1=x_sb[u][:, i, :], op=ALU.add
                 )
-            nc.sync.dma_start(out=unit_rows(out_rows, u), in_=result[:])
+            stores = UNIT_TILES if u == UNITS - 1 else 1
+            tiles = UNIT_TILES // stores
+            for i in range(0, UNIT_TILES, tiles):
+                nc.sync.dma_start(
+                    out=unit_rows(out_rows, u)[:, i : i + tiles, :], in_=result[:, i : i + tiles, :]
+                )
 
         def has_pair(n):
             return live(n + X_AHEAD) or live(n - G_BEHIND)
@@ -204,18 +215,22 @@ def tile_hydraencoderlayer_pb_t_kernel(tc, x, wq, kv, wo, out):
                 inverse_norms(n + 1)
             if has_pair(n):
                 transpose_pair(n)
-            if live(n - 4):
-                finish(n - 4)
-            if has_pair(n - 1):
+            draining = n >= UNITS
+            if has_pair(n - 1) and draining:
+                quantise_pair(n - 1)
+            if live(n - 3):
+                finish(n - 3)
+            if has_pair(n - 1) and not draining:
                 quantise_pair(n - 1)
             if live(n):
                 gate(n)
-            if live(n - 3):
-                o_of[n - 3] = multiply_unit(mx_of[n - 2], G_HALF, wo_mx, o_psum, "o")
+            if live(n - 2):
+                pool, tag = (a_psum, "a") if n - 2 == UNITS - 1 else (o_psum, "o")
+                o_of[n - 2] = multiply_unit(mx_of[n - 1], G_HALF, wo_mx, pool, tag)
 
         wq_mx = quantise_weight(wq_raw, "wq")
         for n in range(-X_AHEAD, -1):
             step(n)
         wo_mx = quantise_weight(wo_raw, "wo")
-        for n in range(-1, UNITS + 4):
+        for n in range(-1, UNITS + 3):
             step(n)

@@ -25,7 +25,7 @@ UNITS = B * S // UNIT_TOKENS
 X_AHEAD = 3
 G_BEHIND = 1
 LOAD_UNITS = 4
-WARM_UP = 4
+WARM_UP = 3
 X_HALF = 0
 G_HALF = 1
 
@@ -57,12 +57,8 @@ def tile_hydraencoderlayer_pb_t_kernel(tc, x, wq, kv, wo, out):
             )
             return raw
 
-        kv_sb = {}
-
-        def load_kv(b):
-            kv_row = keep.tile([P, DI], BF16, name="kv%d" % b)
-            nc.sync.dma_start(out=kv_row[:], in_=kv[b, 0, :].partition_broadcast(P))
-            kv_sb[b] = kv_row
+        kv_rows = keep.tile([P, DI], BF16, name="kv_rows")
+        nc.vector.memset(kv_rows[:].bitcast(U32), 0)
 
         x_sb = {}
 
@@ -73,14 +69,12 @@ def tile_hydraencoderlayer_pb_t_kernel(tc, x, wq, kv, wo, out):
                 x_sb[u + i] = x_units[:, i * UNIT_TILES : (i + 1) * UNIT_TILES, :]
 
         wq_raw = load_weight(wq, "wq_raw")
+        nc.sync.dma_start(out=kv_rows[:B, :], in_=kv.rearrange("b o e -> (b o) e"))
         load_x(0)
         load_x(1)
-        load_kv(0)
         wo_raw = load_weight(wo, "wo_raw")
         load_x(2, units=2)
         for u in range(LOAD_UNITS, UNITS, LOAD_UNITS):
-            if u * UNIT_TOKENS % S == 0:
-                load_kv(u * UNIT_TOKENS // S)
             load_x(u, units=LOAD_UNITS)
 
         identity = keep.tile([P, P], F32, name="identity")
@@ -88,11 +82,32 @@ def tile_hydraencoderlayer_pb_t_kernel(tc, x, wq, kv, wo, out):
         minus_half = keep.tile([P, UNIT_TILES], F32, name="minus_half")
         nc.gpsimd.memset(minus_half[:], -0.5)
 
+        kv_selector = keep.tile([P, B], BF16, name="kv_selector")
+        nc.vector.tensor_copy(out=kv_selector[:], in_=identity[:, :B])
+        kv_bank, kv_sb = {}, {}
+
+        def broadcast_kv(b):
+            kv_bank[b] = o_psum.tile([P, DI], F32, name="kv_bank", tag="o")
+            nc.tensor.matmul(
+                kv_bank[b][:],
+                lhsT=kv_selector[:, b : b + 1].to_broadcast([P, P]),
+                rhs=kv_rows[:],
+                start=True,
+                stop=True,
+            )
+
+        def keep_kv(copy, b):
+            kv_sb[b] = keep.tile([P, DI], BF16, name="kv%d" % b)
+            copy(out=kv_sb[b][:], in_=kv_bank[b][:])
+
         zeros = keep.tile([P, DI], BF16, name="zeros")
-        nc.vector.memset(zeros[:], 0.0)
+        nc.vector.memset(zeros[:].bitcast(U32), 0)
         for i in range(WARM_UP):
             warm = o_psum.tile([P, DI], F32, name="warm", tag="o")
             nc.tensor.matmul(warm[:], lhsT=zeros[:, :P], rhs=zeros[:], start=True, stop=True)
+
+        broadcast_kv(0)
+        keep_kv(nc.scalar.copy, 0)
 
         def quantise_weight(raw, name):
             n = raw.shape[2]
@@ -231,6 +246,12 @@ def tile_hydraencoderlayer_pb_t_kernel(tc, x, wq, kv, wo, out):
         wq_mx = quantise_weight(wq_raw, "wq")
         for n in range(-X_AHEAD, -1):
             step(n)
+        broadcast_kv(1)
+        keep_kv(nc.scalar.copy, 1)
         wo_mx = quantise_weight(wo_raw, "wo")
-        for n in range(-1, UNITS + 3):
+        step(-1)
+        for b in (2, 3):
+            broadcast_kv(b)
+            keep_kv(nc.vector.tensor_copy, b)
+        for n in range(UNITS + 3):
             step(n)

@@ -26,6 +26,7 @@ X_AHEAD = 3
 G_BEHIND = 1
 LOAD_UNITS = 4
 WARM_UP = 3
+V_COLS = 384
 X_HALF = 0
 G_HALF = 1
 
@@ -107,7 +108,8 @@ def tile_hydraencoderlayer_pb_t_kernel(tc, x, wq, kv, wo, out):
             nc.tensor.matmul(warm[:], lhsT=zeros[:, :P], rhs=zeros[:], start=True, stop=True)
 
         broadcast_kv(0)
-        keep_kv(nc.scalar.copy, 0)
+
+        pace = keep.tile([P, 1], BF16, name="pace")
 
         def quantise_weight(raw, name):
             n = raw.shape[2]
@@ -123,7 +125,7 @@ def tile_hydraencoderlayer_pb_t_kernel(tc, x, wq, kv, wo, out):
             return codes, scales
 
         grouped_of, mx_of = {}, {}
-        a_of, inv_norm_of, g_of, o_of = {}, {}, {}, {}
+        a_of, inv_norm_of, g_of, o_of, result_of = {}, {}, {}, {}, {}
 
         def live(u):
             return 0 <= u < UNITS
@@ -208,11 +210,22 @@ def tile_hydraencoderlayer_pb_t_kernel(tc, x, wq, kv, wo, out):
                 )
             g_of[u] = g
 
+        def start_finish(n, u):
+            result = results.tile([P, UNIT_TILES, D], F32, name="result", tag="result")
+            result_of[u] = result
+            i = UNIT_TILES - 1
+            nc.scalar.copy(out=result[:, i, V_COLS:], in_=o_of[u][i][:, V_COLS:])
+            if live(n - 1):
+                nc.gpsimd.tensor_copy(out=pace[:], in_=g_of[n - 1][:, i, DI - 1 : DI])
+            nc.gpsimd.tensor_tensor(
+                out=result[:, i, V_COLS:], in0=result[:, i, V_COLS:], in1=x_sb[u][:, i, V_COLS:], op=ALU.add
+            )
+
         def finish(u):
-            result = results.tile([P, UNIT_TILES, D], F32, tag="result")
-            for i in range(UNIT_TILES):
+            result = result_of[u]
+            for i, cols in enumerate((D, V_COLS)):
                 nc.vector.tensor_tensor(
-                    out=result[:, i, :], in0=o_of[u][i][:], in1=x_sb[u][:, i, :], op=ALU.add
+                    out=result[:, i, :cols], in0=o_of[u][i][:, :cols], in1=x_sb[u][:, i, :cols], op=ALU.add
                 )
             stores = UNIT_TILES if u == UNITS - 1 else 1
             tiles = UNIT_TILES // stores
@@ -225,6 +238,8 @@ def tile_hydraencoderlayer_pb_t_kernel(tc, x, wq, kv, wo, out):
             return live(n + X_AHEAD) or live(n - G_BEHIND)
 
         def step(n):
+            if live(n - 3):
+                start_finish(n, n - 3)
             if live(n + 1):
                 a_of[n + 1] = multiply_unit(mx_of[n - 2], X_HALF, wq_mx, a_psum, "a")
                 inverse_norms(n + 1)
@@ -246,12 +261,14 @@ def tile_hydraencoderlayer_pb_t_kernel(tc, x, wq, kv, wo, out):
         wq_mx = quantise_weight(wq_raw, "wq")
         for n in range(-X_AHEAD, -1):
             step(n)
-        broadcast_kv(1)
-        keep_kv(nc.scalar.copy, 1)
+        keep_kv(nc.scalar.copy, 0)
         wo_mx = quantise_weight(wo_raw, "wo")
+        broadcast_kv(1)
         step(-1)
-        for b in (2, 3):
-            broadcast_kv(b)
-            keep_kv(nc.vector.tensor_copy, b)
+        keep_kv(nc.scalar.copy, 1)
         for n in range(UNITS + 3):
+            if n in (0, 1):
+                broadcast_kv(2 + n)
             step(n)
+            if n in (0, 1):
+                keep_kv(nc.vector.tensor_copy, 2 + n)

from contextlib import ExitStack

import concourse.mybir as mybir
from concourse.masks import make_identity

F32 = mybir.dt.float32
BF16 = mybir.dt.bfloat16
U32 = mybir.dt.uint32
U8 = mybir.dt.uint8
FP8X4 = mybir.dt.float8_e4m3fn_x4
ACT = mybir.ActivationFunctionType
ALU = mybir.AluOpType

B, S, D, DI = 4, 2048, 512, 512
EPS = 1e-12
FLOPS = 2 * B * S * D * DI + 2 * B * S * DI * D

P = 128
PACK = 4
HALVES = 2
TILES_PER_BATCH = S // P
UNIT_TILES = 2
UNIT_TOKENS = UNIT_TILES * P
UNITS = B * S // UNIT_TOKENS
X_AHEAD = 3
G_BEHIND = 1
LOAD_UNITS = 4
WARM_UP = 3
V_COLS = 384
X_HALF = 0
G_HALF = 1


def tile_hydraencoderlayer_pb_t_kernel(tc, x, wq, kv, wo, out):
    nc = tc.nc
    x_rows = x.flatten_outer_dims()
    out_rows = out.flatten_outer_dims()

    def unit_rows(rows, u, units=1):
        b, first_tile = divmod(u * UNIT_TILES, TILES_PER_BATCH)
        batch = rows[b * S : (b + 1) * S, :].rearrange("(p t) d -> p t d", t=TILES_PER_BATCH)
        return batch[:, first_tile : first_tile + units * UNIT_TILES, :]

    with ExitStack() as stack:
        stack.enter_context(tc.manual_schedule())
        keep = stack.enter_context(tc.tile_pool(name="keep", bufs=1))
        stream = stack.enter_context(tc.tile_pool(name="stream", bufs=3))
        results = stack.enter_context(tc.tile_pool(name="results", bufs=4))
        words_psum = stack.enter_context(tc.psum_pool(name="words_psum", bufs=2))
        a_psum = stack.enter_context(tc.psum_pool(name="a_psum", bufs=2 * UNIT_TILES))
        o_psum = stack.enter_context(tc.psum_pool(name="o_psum", bufs=UNIT_TILES))

        def load_weight(w, name):
            raw = keep.tile([P, PACK, w.shape[1]], BF16, name=name)
            nc.sync.dma_start(
                out=raw[:].rearrange("p (h e) n -> p h (e n)", h=HALVES),
                in_=w.rearrange("(h p e) n -> p h (e n)", h=HALVES, p=P),
            )
            return raw

        kv_rows = keep.tile([P, DI], BF16, name="kv_rows")
        nc.vector.memset(kv_rows[:].bitcast(U32), 0)

        x_sb = {}

        def load_x(u, units=1):
            x_units = keep.tile([P, units * UNIT_TILES, D], BF16, name="x%d" % u)
            nc.sync.dma_start(out=x_units[:], in_=unit_rows(x_rows, u, units))
            for i in range(units):
                x_sb[u + i] = x_units[:, i * UNIT_TILES : (i + 1) * UNIT_TILES, :]

        wq_raw = load_weight(wq, "wq_raw")
        nc.sync.dma_start(out=kv_rows[:B, :], in_=kv.rearrange("b o e -> (b o) e"))
        load_x(0)
        load_x(1)
        wo_raw = load_weight(wo, "wo_raw")
        load_x(2, units=2)
        for u in range(LOAD_UNITS, UNITS, LOAD_UNITS):
            load_x(u, units=LOAD_UNITS)

        identity = keep.tile([P, P], F32, name="identity")
        make_identity(nc, identity[:])
        minus_half = keep.tile([P, UNIT_TILES], F32, name="minus_half")
        nc.gpsimd.memset(minus_half[:], -0.5)

        kv_selector = keep.tile([P, B], BF16, name="kv_selector")
        nc.vector.tensor_copy(out=kv_selector[:], in_=identity[:, :B])
        kv_bank, kv_sb = {}, {}

        def broadcast_kv(b):
            kv_bank[b] = o_psum.tile([P, DI], F32, name="kv_bank", tag="o")
            nc.tensor.matmul(
                kv_bank[b][:],
                lhsT=kv_selector[:, b : b + 1].to_broadcast([P, P]),
                rhs=kv_rows[:],
                start=True,
                stop=True,
            )

        def keep_kv(copy, b):
            kv_sb[b] = keep.tile([P, DI], BF16, name="kv%d" % b)
            copy(out=kv_sb[b][:], in_=kv_bank[b][:])

        zeros = keep.tile([P, DI], BF16, name="zeros")
        nc.vector.memset(zeros[:].bitcast(U32), 0)
        for i in range(WARM_UP):
            warm = o_psum.tile([P, DI], F32, name="warm", tag="o")
            nc.tensor.matmul(warm[:], lhsT=zeros[:, :P], rhs=zeros[:], start=True, stop=True)

        broadcast_kv(0)

        pace = keep.tile([P, 1], BF16, name="pace")

        def quantise_weight(raw, name):
            n = raw.shape[2]
            grouped = keep.tile([P, n, PACK], BF16, name=name + "_grouped", align_bytes=64)
            nc.vector.tensor_copy(out=grouped[:], in_=raw[:].rearrange("p t n -> p n t"))
            codes = keep.tile([P, n], U32, name=name + "_codes", align_bytes=64)
            scales = keep.tile([P, n], U8, name=name + "_scales", align_bytes=64)
            nc.vector.quantize_mx(
                out=codes[:].bitcast(FP8X4),
                scales=scales[:],
                in_=grouped[:].rearrange("p n t -> p (n t)"),
            )
            return codes, scales

        grouped_of, mx_of = {}, {}
        a_of, inv_norm_of, g_of, o_of, result_of = {}, {}, {}, {}, {}

        def live(u):
            return 0 <= u < UNITS

        def transpose_unit(rows_sb, grouped_half):
            words = rows_sb.bitcast(F32)
            bank = words_psum.tile([P, HALVES, UNIT_TOKENS], F32, tag="words")
            for i in range(UNIT_TILES):
                for h in range(HALVES):
                    nc.tensor.transpose(
                        bank[:, h, i * P : (i + 1) * P], words[:, i, h * P : (h + 1) * P], identity[:]
                    )
            nc.scalar.copy(
                out=grouped_half.bitcast(F32).rearrange("p (c h) -> p c h", h=HALVES),
                in_=bank[:].rearrange("p h c -> p c h"),
            )

        def transpose_pair(n):
            grouped = stream.tile([P, 2, UNIT_TOKENS * PACK], BF16, tag="grouped", align_bytes=64)
            if live(n - G_BEHIND):
                transpose_unit(g_of[n - G_BEHIND][:], grouped[:, G_HALF, :])
            if live(n + X_AHEAD):
                transpose_unit(x_sb[n + X_AHEAD], grouped[:, X_HALF, :])
            grouped_of[n] = grouped

        def quantise_pair(n):
            codes = stream.tile([P, 2, UNIT_TOKENS], U32, tag="codes", align_bytes=64)
            scales = stream.tile([P, 2, UNIT_TOKENS], U8, tag="scales", align_bytes=64)
            first = X_HALF if live(n + X_AHEAD) else G_HALF
            last = G_HALF if live(n - G_BEHIND) else X_HALF
            filled = slice(first, last + 1)
            nc.vector.quantize_mx(
                out=codes[:, filled, :].rearrange("p s c -> p (s c)").bitcast(FP8X4),
                scales=scales[:, filled, :].rearrange("p s c -> p (s c)"),
                in_=grouped_of[n][:, filled, :].rearrange("p s c -> p (s c)"),
            )
            mx_of[n] = (codes, scales)

        def multiply_unit(operand, half, weight, psum_pool, tag):
            codes, scales = operand
            w_codes, w_scales = weight
            banks = []
            for i in range(UNIT_TILES):
                tokens = slice(i * P, (i + 1) * P)
                acc = psum_pool.tile([P, w_codes.shape[1]], F32, tag=tag)
                nc.tensor.matmul_mx(
                    out=acc[:],
                    lhsT=codes[:, half, tokens].bitcast(FP8X4),
                    lhsT_scale=scales[:, half, tokens],
                    rhs=w_codes[:].bitcast(FP8X4),
                    rhs_scale=w_scales[:],
                    start=True,
                    stop=True,
                )
                banks.append(acc)
            return banks

        def inverse_norms(u):
            sums = stream.tile([P, UNIT_TILES], F32, tag="sums")
            for i in range(UNIT_TILES):
                squares = stream.tile([P, DI], BF16, tag="squares")
                nc.scalar.activation(
                    out=squares[:], in_=a_of[u][i][:], func=ACT.Square, accum_out=sums[:, i : i + 1]
                )
            clamped = stream.tile([P, UNIT_TILES], F32, tag="clamped")
            nc.gpsimd.tensor_scalar_max(out=clamped[:], in0=sums[:], scalar1=EPS * EPS)
            inv_norm = stream.tile([P, UNIT_TILES], F32, tag="inv_norm")
            nc.gpsimd.tensor_tensor(out=inv_norm[:], in0=clamped[:], in1=minus_half[:], op=ALU.pow)
            inv_norm_of[u] = inv_norm

        def gate(u):
            b = u * UNIT_TOKENS // S
            g = stream.tile([P, UNIT_TILES, DI], BF16, tag="g")
            for i in range(UNIT_TILES):
                nc.vector.scalar_tensor_tensor(
                    out=g[:, i, :],
                    in0=a_of[u][i][:],
                    scalar=inv_norm_of[u][:, i : i + 1],
                    in1=kv_sb[b][:],
                    op0=ALU.mult,
                    op1=ALU.mult,
                )
            g_of[u] = g

        def start_finish(n, u):
            result = results.tile([P, UNIT_TILES, D], F32, name="result", tag="result")
            result_of[u] = result
            i = UNIT_TILES - 1
            nc.scalar.copy(out=result[:, i, V_COLS:], in_=o_of[u][i][:, V_COLS:])
            if live(n - 1):
                nc.gpsimd.tensor_copy(out=pace[:], in_=g_of[n - 1][:, i, DI - 1 : DI])
            nc.gpsimd.tensor_tensor(
                out=result[:, i, V_COLS:], in0=result[:, i, V_COLS:], in1=x_sb[u][:, i, V_COLS:], op=ALU.add
            )

        def finish(u):
            result = result_of[u]
            for i, cols in enumerate((D, V_COLS)):
                nc.vector.tensor_tensor(
                    out=result[:, i, :cols], in0=o_of[u][i][:, :cols], in1=x_sb[u][:, i, :cols], op=ALU.add
                )
            stores = UNIT_TILES if u == UNITS - 1 else 1
            tiles = UNIT_TILES // stores
            for i in range(0, UNIT_TILES, tiles):
                nc.sync.dma_start(
                    out=unit_rows(out_rows, u)[:, i : i + tiles, :], in_=result[:, i : i + tiles, :]
                )

        def has_pair(n):
            return live(n + X_AHEAD) or live(n - G_BEHIND)

        def step(n):
            if live(n - 3):
                start_finish(n, n - 3)
            if live(n + 1):
                a_of[n + 1] = multiply_unit(mx_of[n - 2], X_HALF, wq_mx, a_psum, "a")
                inverse_norms(n + 1)
            if has_pair(n):
                transpose_pair(n)
            draining = n >= UNITS
            if has_pair(n - 1) and draining:
                quantise_pair(n - 1)
            if live(n - 3):
                finish(n - 3)
            if has_pair(n - 1) and not draining:
                quantise_pair(n - 1)
            if live(n):
                gate(n)
            if live(n - 2):
                pool, tag = (a_psum, "a") if n - 2 == UNITS - 1 else (o_psum, "o")
                o_of[n - 2] = multiply_unit(mx_of[n - 1], G_HALF, wo_mx, pool, tag)

        wq_mx = quantise_weight(wq_raw, "wq")
        for n in range(-X_AHEAD, -1):
            step(n)
        keep_kv(nc.scalar.copy, 0)
        wo_mx = quantise_weight(wo_raw, "wo")
        broadcast_kv(1)
        step(-1)
        keep_kv(nc.scalar.copy, 1)
        for n in range(UNITS + 3):
            if n in (0, 1):
                broadcast_kv(2 + n)
            step(n)
            if n in (0, 1):
                keep_kv(nc.vector.tensor_copy, 2 + n)
